import numpy as np
import ml_dtypes

BF16 = ml_dtypes.bfloat16


def bf(x):
    return np.asarray(x, np.float32).astype(BF16)


def f32(x):
    return np.asarray(x, np.float32)


def f64(x):
    return np.asarray(x).astype(np.float64)


def striped(idx):
    return np.tile(idx.reshape(-1, 16).T, (8, 1))


C, S, N, RB = 512, 256, 128, 128
CUTOFF = 8.0
WIDTH = 0.5 * CUTOFF / RB


def setup_inputs():
    return {
        "x": f32(np.random.standard_normal((C, S))),
        "lig": f32(np.random.standard_normal((C, N))),
        "dist": f32(np.random.uniform(0.5, 7.5, (1, N))),
        "centers": f32(np.linspace(0.0, CUTOFF, RB).reshape(RB, 1)),
        "w1r": bf(0.5 * np.random.standard_normal((RB, C))),
        "b1": f32(0.1 * np.random.standard_normal((C, 1))),
        "w2": bf(np.random.standard_normal((C, C)) / np.sqrt(C)),
        "b2": f32(0.1 * np.random.standard_normal((C, 1))),
        "offs": striped(np.random.permutation(np.tile(np.arange(S), 2))[:N]),
    }


def reference(x, lig, dist, centers, w1r, b1, w2, b2, offs):
    idx = offs[:16].T.reshape(-1)
    rb = np.exp(-0.5 * ((f64(dist) - f64(centers)) / (WIDTH + 1e-8)) ** 2)
    u = f64(x)[:, idx] + f64(lig)
    h1 = np.maximum(u + f64(w1r).T @ rb + f64(b1), 0.0)
    return np.maximum(f64(w2).T @ h1 + f64(b2), 0.0)

@@ -1,0 +1,77 @@
+import concourse.mybir as mybir
+
+P = 128
+C, S, N, RB = 512, 256, 128, 128
+CB = C // P
+
+F32, BF16, U16 = mybir.dt.float32, mybir.dt.bfloat16, mybir.dt.uint16
+ADD, MAX = mybir.AluOpType.add, mybir.AluOpType.max
+SQUARE = mybir.ActivationFunctionType.Square
+EXP = mybir.ActivationFunctionType.Exp
+RELU = mybir.ActivationFunctionType.Relu
+
+BIN_WIDTH = 0.03125 + 1e-8
+EXP_SCALE = -0.5 / (BIN_WIDTH * BIN_WIDTH)
+
+FLOPS = 2 * N * (RB * C + C * C)
+
+
+def tile_dockingscorepredictor_kernel(tc, x, lig, dist, centers, w1r, b1, w2, b2, offs, out):
+    nc = tc.nc
+    with (
+        tc.tile_pool(name="held", bufs=1) as held,
+        tc.psum_pool(name="psum", bufs=1) as psum,
+    ):
+        offsets = held.tile([P, N // 16], U16, name="offsets")
+        nc.sync.dma_start(offsets[:], offs)
+
+        dist_all = held.tile([P, N], F32, name="dist_all")
+        nc.sync.dma_start(dist_all[:], dist.broadcast_to([P, N]))
+        centers_sb = held.tile([P, 1], F32, name="centers_sb")
+        nc.scalar.dma_start(centers_sb[:], centers)
+        w1r_sb = held.tile([P, C], BF16, name="w1r_sb")
+        nc.scalar.dma_start(w1r_sb[:], w1r)
+
+        x_sb = [held.tile([P, S], F32, name=f"x_sb{b}") for b in range(CB)]
+        lig_sb = [held.tile([P, N], F32, name=f"lig_sb{b}") for b in range(CB)]
+        for b in range(CB):
+            nc.sync.dma_start(x_sb[b][:], x[b * P : (b + 1) * P, :])
+            nc.scalar.dma_start(lig_sb[b][:], lig[b * P : (b + 1) * P, :])
+
+        b1_sb = held.tile([P, CB], F32, name="b1_sb")
+        b2_sb = held.tile([P, CB], F32, name="b2_sb")
+        with nc.allow_non_contiguous_dma(reason="a bias vector, one element to a partition"):
+            nc.gpsimd.dma_start(b1_sb[:], b1.rearrange("(b p) o -> p (b o)", p=P))
+            nc.gpsimd.dma_start(b2_sb[:], b2.rearrange("(b p) o -> p (b o)", p=P))
+
+        w2_sb = [held.tile([P, C], BF16, name=f"w2_sb{k}") for k in range(CB)]
+        for k in range(CB):
+            nc.gpsimd.dma_start(w2_sb[k][:], w2[k * P : (k + 1) * P, :])
+
+        sq = held.tile([P, N], F32, name="sq")
+        nc.scalar.activation(sq[:], dist_all[:], SQUARE, bias=centers_sb[:, 0:1], scale=-1.0)
+        rb = held.tile([P, N], BF16, name="rb")
+        nc.scalar.activation(rb[:], sq[:], EXP, scale=EXP_SCALE)
+
+        h1 = [held.tile([P, N], BF16, name=f"h1_{b}") for b in range(CB)]
+        for b in range(CB):
+            u = held.tile([P, N], F32, name=f"u{b}")
+            nc.vector.tensor_tensor(u[:], x_sb[b][:].indirect(offsets[:]), lig_sb[b][:], ADD)
+
+            radial = psum.tile([P, N], F32, name=f"radial{b}")
+            nc.tensor.matmul(radial[:], w1r_sb[:, b * P : (b + 1) * P], rb[:], start=True, stop=True)
+
+            pre = held.tile([P, N], F32, name=f"pre{b}")
+            nc.vector.tensor_tensor(pre[:], radial[:], u[:], ADD)
+            nc.scalar.activation(h1[b][:], pre[:], RELU, bias=b1_sb[:, b : b + 1])
+
+        acc = [psum.tile([P, N], F32, name=f"acc{m}") for m in range(CB)]
+        for k in range(CB):
+            for m in range(CB):
+                nc.tensor.matmul(
+                    acc[m][:], w2_sb[k][:, m * P : (m + 1) * P], h1[k][:], start=(k == 0), stop=(k == CB - 1)
+                )
+        for m in range(CB):
+            res = held.tile([P, N], F32, name=f"res{m}")
+            nc.scalar.activation(res[:], acc[m][:], RELU, bias=b2_sb[:, m : m + 1])
+            nc.sync.dma_start(out[m * P : (m + 1) * P, :], res[:])

@@ -5,7 +5,7 @@ C, S, N, RB = 512, 256, 128, 128
 CB = C // P
 
 F32, BF16, U16 = mybir.dt.float32, mybir.dt.bfloat16, mybir.dt.uint16
-ADD, MAX = mybir.AluOpType.add, mybir.AluOpType.max
+ADD = mybir.AluOpType.add
 SQUARE = mybir.ActivationFunctionType.Square
 EXP = mybir.ActivationFunctionType.Exp
 RELU = mybir.ActivationFunctionType.Relu
@@ -32,21 +32,22 @@ def tile_dockingscorepredictor_kernel(tc, x, lig, dist, centers, w1r, b1, w2, b2
         w1r_sb = held.tile([P, C], BF16, name="w1r_sb")
         nc.scalar.dma_start(w1r_sb[:], w1r)
 
-        x_sb = [held.tile([P, S], F32, name=f"x_sb{b}") for b in range(CB)]
-        lig_sb = [held.tile([P, N], F32, name=f"lig_sb{b}") for b in range(CB)]
-        for b in range(CB):
-            nc.sync.dma_start(x_sb[b][:], x[b * P : (b + 1) * P, :])
-            nc.scalar.dma_start(lig_sb[b][:], lig[b * P : (b + 1) * P, :])
-
         b1_sb = held.tile([P, CB], F32, name="b1_sb")
         b2_sb = held.tile([P, CB], F32, name="b2_sb")
         with nc.allow_non_contiguous_dma(reason="a bias vector, one element to a partition"):
-            nc.gpsimd.dma_start(b1_sb[:], b1.rearrange("(b p) o -> p (b o)", p=P))
-            nc.gpsimd.dma_start(b2_sb[:], b2.rearrange("(b p) o -> p (b o)", p=P))
+            nc.scalar.dma_start(b1_sb[:], b1.rearrange("(b p) o -> p (b o)", p=P))
 
+        x_sb = [held.tile([P, S], F32, name=f"x_sb{b}") for b in range(CB)]
+        lig_sb = [held.tile([P, N], F32, name=f"lig_sb{b}") for b in range(CB)]
         w2_sb = [held.tile([P, C], BF16, name=f"w2_sb{k}") for k in range(CB)]
+        queues = [nc.sync, nc.scalar]
+        for b in range(CB):
+            queues[b % 2].dma_start(x_sb[b][:], x[b * P : (b + 1) * P, :])
+            queues[(b + 1) % 2].dma_start(lig_sb[b][:], lig[b * P : (b + 1) * P, :])
         for k in range(CB):
-            nc.gpsimd.dma_start(w2_sb[k][:], w2[k * P : (k + 1) * P, :])
+            queues[k % 2].dma_start(w2_sb[k][:], w2[k * P : (k + 1) * P, :])
+        with nc.allow_non_contiguous_dma(reason="a bias vector, one element to a partition"):
+            nc.sync.dma_start(b2_sb[:], b2.rearrange("(b p) o -> p (b o)", p=P))
 
         sq = held.tile([P, N], F32, name="sq")
         nc.scalar.activation(sq[:], dist_all[:], SQUARE, bias=centers_sb[:, 0:1], scale=-1.0)

@@ -5,7 +5,7 @@ C, S, N, RB = 512, 256, 128, 128
 CB = C // P
 
 F32, BF16, U16 = mybir.dt.float32, mybir.dt.bfloat16, mybir.dt.uint16
-ADD = mybir.AluOpType.add
+ADD, MAX = mybir.AluOpType.add, mybir.AluOpType.max
 SQUARE = mybir.ActivationFunctionType.Square
 EXP = mybir.ActivationFunctionType.Exp
 RELU = mybir.ActivationFunctionType.Relu
@@ -25,54 +25,57 @@ def tile_dockingscorepredictor_kernel(tc, x, lig, dist, centers, w1r, b1, w2, b2
         offsets = held.tile([P, N // 16], U16, name="offsets")
         nc.sync.dma_start(offsets[:], offs)
 
-        dist_all = held.tile([P, N], F32, name="dist_all")
-        nc.sync.dma_start(dist_all[:], dist.broadcast_to([P, N]))
         centers_sb = held.tile([P, 1], F32, name="centers_sb")
         nc.scalar.dma_start(centers_sb[:], centers)
         w1r_sb = held.tile([P, C], BF16, name="w1r_sb")
         nc.scalar.dma_start(w1r_sb[:], w1r)
-
         b1_sb = held.tile([P, CB], F32, name="b1_sb")
+        nc.scalar.dma_start(b1_sb[:], b1.rearrange("(p b) o -> p (b o)", b=CB))
+        lig_sb = held.tile([P, CB, N], F32, name="lig_sb")
+        nc.scalar.dma_start(lig_sb[:], lig.rearrange("(p b) j -> p b j", b=CB))
         b2_sb = held.tile([P, CB], F32, name="b2_sb")
-        with nc.allow_non_contiguous_dma(reason="a bias vector, one element to a partition"):
-            nc.scalar.dma_start(b1_sb[:], b1.rearrange("(b p) o -> p (b o)", p=P))
+        nc.scalar.dma_start(b2_sb[:], b2.rearrange("(p b) o -> p (b o)", b=CB))
 
+        dist_all = held.tile([P, N], F32, name="dist_all")
+        nc.sync.dma_start(dist_all[:], dist.broadcast_to([P, N]))
+        x_blocks = x.rearrange("(p b) s -> b p s", b=CB)
         x_sb = [held.tile([P, S], F32, name=f"x_sb{b}") for b in range(CB)]
-        lig_sb = [held.tile([P, N], F32, name=f"lig_sb{b}") for b in range(CB)]
-        w2_sb = [held.tile([P, C], BF16, name=f"w2_sb{k}") for k in range(CB)]
-        queues = [nc.sync, nc.scalar]
         for b in range(CB):
-            queues[b % 2].dma_start(x_sb[b][:], x[b * P : (b + 1) * P, :])
-            queues[(b + 1) % 2].dma_start(lig_sb[b][:], lig[b * P : (b + 1) * P, :])
+            nc.sync.dma_start(x_sb[b][:], x_blocks[b])
+        w2_blocks = w2.rearrange("(p k) m -> k p m", k=CB)
+        w2_sb = [held.tile([P, C], BF16, name=f"w2_sb{k}") for k in range(CB)]
         for k in range(CB):
-            queues[k % 2].dma_start(w2_sb[k][:], w2[k * P : (k + 1) * P, :])
-        with nc.allow_non_contiguous_dma(reason="a bias vector, one element to a partition"):
-            nc.sync.dma_start(b2_sb[:], b2.rearrange("(b p) o -> p (b o)", p=P))
+            nc.sync.dma_start(w2_sb[k][:], w2_blocks[k])
 
         sq = held.tile([P, N], F32, name="sq")
         nc.scalar.activation(sq[:], dist_all[:], SQUARE, bias=centers_sb[:, 0:1], scale=-1.0)
         rb = held.tile([P, N], BF16, name="rb")
         nc.scalar.activation(rb[:], sq[:], EXP, scale=EXP_SCALE)
 
+        w1r_by_block = w1r_sb[:].rearrange("r (p b) -> r b p", b=CB)
+        radial = psum.tile([P, CB, N], F32, name="radial")
+        for b in range(CB):
+            nc.tensor.matmul(radial[:, b, :], w1r_by_block[:, b, :], rb[:], start=True, stop=True)
+
         h1 = [held.tile([P, N], BF16, name=f"h1_{b}") for b in range(CB)]
         for b in range(CB):
             u = held.tile([P, N], F32, name=f"u{b}")
-            nc.vector.tensor_tensor(u[:], x_sb[b][:].indirect(offsets[:]), lig_sb[b][:], ADD)
-
-            radial = psum.tile([P, N], F32, name=f"radial{b}")
-            nc.tensor.matmul(radial[:], w1r_sb[:, b * P : (b + 1) * P], rb[:], start=True, stop=True)
-
+            nc.vector.tensor_tensor(u[:], x_sb[b][:].indirect(offsets[:]), lig_sb[:, b, :], ADD)
             pre = held.tile([P, N], F32, name=f"pre{b}")
-            nc.vector.tensor_tensor(pre[:], radial[:], u[:], ADD)
+            nc.vector.tensor_tensor(pre[:], radial[:, b, :], u[:], ADD)
             nc.scalar.activation(h1[b][:], pre[:], RELU, bias=b1_sb[:, b : b + 1])
 
         acc = [psum.tile([P, N], F32, name=f"acc{m}") for m in range(CB)]
         for k in range(CB):
+            w2_by_block = w2_sb[k][:].rearrange("c (q m) -> c m q", m=CB)
             for m in range(CB):
-                nc.tensor.matmul(
-                    acc[m][:], w2_sb[k][:, m * P : (m + 1) * P], h1[k][:], start=(k == 0), stop=(k == CB - 1)
-                )
-        for m in range(CB):
-            res = held.tile([P, N], F32, name=f"res{m}")
-            nc.scalar.activation(res[:], acc[m][:], RELU, bias=b2_sb[:, m : m + 1])
-            nc.sync.dma_start(out[m * P : (m + 1) * P, :], res[:])
+                nc.tensor.matmul(acc[m][:], w2_by_block[:, m, :], h1[k][:], start=(k == 0), stop=(k == CB - 1))
+
+        out_blocks = out.rearrange("(q m) j -> q m j", m=CB)
+        stores = [nc.sync, nc.scalar]
+        for half in range(CB // 2):
+            res = held.tile([P, 2, N], F32, name=f"res{half}")
+            m = 2 * half
+            nc.scalar.activation(res[:, 0, :], acc[m][:], RELU, bias=b2_sb[:, m : m + 1])
+            nc.vector.tensor_scalar(res[:, 1, :], acc[m + 1][:], b2_sb[:, m + 1 : m + 2], 0.0, ADD, MAX)
+            stores[half].dma_start(out_blocks[:, m : m + 2, :], res[:])

@@ -15,6 +15,9 @@ EXP_SCALE = -0.5 / (BIN_WIDTH * BIN_WIDTH)
 
 FLOPS = 2 * N * (RB * C + C * C)
 
+BANK = 512
+WARM_UP = 6
+
 
 def tile_dockingscorepredictor_kernel(tc, x, lig, dist, centers, w1r, b1, w2, b2, offs, out):
     nc = tc.nc
@@ -46,6 +49,12 @@ def tile_dockingscorepredictor_kernel(tc, x, lig, dist, centers, w1r, b1, w2, b2
         w2_sb = [held.tile([P, C], BF16, name=f"w2_sb{k}") for k in range(CB)]
         for k in range(CB):
             nc.sync.dma_start(w2_sb[k][:], w2_blocks[k])
+
+        zeros = held.tile([P, BANK], BF16, name="zeros")
+        nc.vector.memset(zeros[:], 0.0)
+        unread = psum.tile([P, BANK], F32, name="unread")
+        for i in range(WARM_UP):
+            nc.tensor.matmul(unread[:], zeros[:, 0:P], zeros[:], start=True, stop=True)
 
         sq = held.tile([P, N], F32, name="sq")
         nc.scalar.activation(sq[:], dist_all[:], SQUARE, bias=centers_sb[:, 0:1], scale=-1.0)

@@ -15,9 +15,6 @@ EXP_SCALE = -0.5 / (BIN_WIDTH * BIN_WIDTH)
 
 FLOPS = 2 * N * (RB * C + C * C)
 
-BANK = 512
-WARM_UP = 6
-
 
 def tile_dockingscorepredictor_kernel(tc, x, lig, dist, centers, w1r, b1, w2, b2, offs, out):
     nc = tc.nc
@@ -28,8 +25,13 @@ def tile_dockingscorepredictor_kernel(tc, x, lig, dist, centers, w1r, b1, w2, b2
         offsets = held.tile([P, N // 16], U16, name="offsets")
         nc.sync.dma_start(offsets[:], offs)
 
-        centers_sb = held.tile([P, 1], F32, name="centers_sb")
-        nc.scalar.dma_start(centers_sb[:], centers)
+        bins_lhsT = held.tile([2, RB], F32, name="bins_lhsT")
+        nc.vector.memset(bins_lhsT[:], 1.0)
+        nc.scalar.dma_start(bins_lhsT[1:2, :], centers.rearrange("r o -> o r"))
+        pairs_rhs = held.tile([2, N], F32, name="pairs_rhs")
+        nc.vector.memset(pairs_rhs[:], -1.0)
+        nc.scalar.dma_start(pairs_rhs[0:1, :], dist)
+
         w1r_sb = held.tile([P, C], BF16, name="w1r_sb")
         nc.scalar.dma_start(w1r_sb[:], w1r)
         b1_sb = held.tile([P, CB], F32, name="b1_sb")
@@ -39,8 +41,6 @@ def tile_dockingscorepredictor_kernel(tc, x, lig, dist, centers, w1r, b1, w2, b2
         b2_sb = held.tile([P, CB], F32, name="b2_sb")
         nc.scalar.dma_start(b2_sb[:], b2.rearrange("(p b) o -> p (b o)", b=CB))
 
-        dist_all = held.tile([P, N], F32, name="dist_all")
-        nc.sync.dma_start(dist_all[:], dist.broadcast_to([P, N]))
         x_blocks = x.rearrange("(p b) s -> b p s", b=CB)
         x_sb = [held.tile([P, S], F32, name=f"x_sb{b}") for b in range(CB)]
         for b in range(CB):
@@ -50,14 +50,10 @@ def tile_dockingscorepredictor_kernel(tc, x, lig, dist, centers, w1r, b1, w2, b2
         for k in range(CB):
             nc.sync.dma_start(w2_sb[k][:], w2_blocks[k])
 
-        zeros = held.tile([P, BANK], BF16, name="zeros")
-        nc.vector.memset(zeros[:], 0.0)
-        unread = psum.tile([P, BANK], F32, name="unread")
-        for i in range(WARM_UP):
-            nc.tensor.matmul(unread[:], zeros[:, 0:P], zeros[:], start=True, stop=True)
-
+        diff = psum.tile([P, N], F32, name="diff")
+        nc.tensor.matmul(diff[:], bins_lhsT[:], pairs_rhs[:], start=True, stop=True)
         sq = held.tile([P, N], F32, name="sq")
-        nc.scalar.activation(sq[:], dist_all[:], SQUARE, bias=centers_sb[:, 0:1], scale=-1.0)
+        nc.scalar.activation(sq[:], diff[:], SQUARE)
         rb = held.tile([P, N], BF16, name="rb")
         nc.scalar.activation(rb[:], sq[:], EXP, scale=EXP_SCALE)
 

@@ -3,6 +3,7 @@ import concourse.mybir as mybir
 P = 128
 C, S, N, RB = 512, 256, 128, 128
 CB = C // P
+BANK = 512
 
 F32, BF16, U16 = mybir.dt.float32, mybir.dt.bfloat16, mybir.dt.uint16
 ADD, MAX = mybir.AluOpType.add, mybir.AluOpType.max
@@ -22,36 +23,46 @@ def tile_dockingscorepredictor_kernel(tc, x, lig, dist, centers, w1r, b1, w2, b2
         tc.tile_pool(name="held", bufs=1) as held,
         tc.psum_pool(name="psum", bufs=1) as psum,
     ):
-        offsets = held.tile([P, N // 16], U16, name="offsets")
-        nc.sync.dma_start(offsets[:], offs)
-
         bins_lhsT = held.tile([2, RB], F32, name="bins_lhsT")
         nc.vector.memset(bins_lhsT[:], 1.0)
-        nc.scalar.dma_start(bins_lhsT[1:2, :], centers.rearrange("r o -> o r"))
         pairs_rhs = held.tile([2, N], F32, name="pairs_rhs")
         nc.vector.memset(pairs_rhs[:], -1.0)
-        nc.scalar.dma_start(pairs_rhs[0:1, :], dist)
+        zeros = held.tile([P, BANK], BF16, name="zeros")
+        nc.vector.memset(zeros[:], 0.0)
 
+        offsets = held.tile([P, N // 16], U16, name="offsets")
+        nc.sync.dma_start(offsets[:], offs)
+        nc.scalar.dma_start(pairs_rhs[0:1, :], dist)
+        nc.scalar.dma_start(bins_lhsT[1:2, :], centers.rearrange("r o -> o r"))
         w1r_sb = held.tile([P, C], BF16, name="w1r_sb")
         nc.scalar.dma_start(w1r_sb[:], w1r)
-        b1_sb = held.tile([P, CB], F32, name="b1_sb")
-        nc.scalar.dma_start(b1_sb[:], b1.rearrange("(p b) o -> p (b o)", b=CB))
-        lig_sb = held.tile([P, CB, N], F32, name="lig_sb")
-        nc.scalar.dma_start(lig_sb[:], lig.rearrange("(p b) j -> p b j", b=CB))
-        b2_sb = held.tile([P, CB], F32, name="b2_sb")
-        nc.scalar.dma_start(b2_sb[:], b2.rearrange("(p b) o -> p (b o)", b=CB))
-
         x_blocks = x.rearrange("(p b) s -> b p s", b=CB)
         x_sb = [held.tile([P, S], F32, name=f"x_sb{b}") for b in range(CB)]
-        for b in range(CB):
+        nc.sync.dma_start(x_sb[0][:], x_blocks[0])
+        lig_sb = held.tile([P, CB, N], F32, name="lig_sb")
+        nc.scalar.dma_start(lig_sb[:], lig.rearrange("(p b) j -> p b j", b=CB))
+        for b in range(1, CB):
             nc.sync.dma_start(x_sb[b][:], x_blocks[b])
         w2_blocks = w2.rearrange("(p k) m -> k p m", k=CB)
         w2_sb = [held.tile([P, C], BF16, name=f"w2_sb{k}") for k in range(CB)]
         for k in range(CB):
             nc.sync.dma_start(w2_sb[k][:], w2_blocks[k])
 
+        b1_sb = held.tile([P, CB], F32, name="b1_sb")
+        nc.gpsimd.dma_start(b1_sb[:], b1.rearrange("(p b) o -> p (b o)", b=CB))
+        b2_sb = held.tile([P, CB], F32, name="b2_sb")
+        nc.gpsimd.dma_start(b2_sb[:], b2.rearrange("(p b) o -> p (b o)", b=CB))
+
+        unread = psum.tile([P, BANK], F32, name="unread")
+
+        def keep_tensor_engine_busy(matmuls):
+            for i in range(matmuls):
+                nc.tensor.matmul(unread[:], zeros[:, 0:P], zeros[:], start=True, stop=True)
+
+        keep_tensor_engine_busy(3)
         diff = psum.tile([P, N], F32, name="diff")
         nc.tensor.matmul(diff[:], bins_lhsT[:], pairs_rhs[:], start=True, stop=True)
+        keep_tensor_engine_busy(1)
         sq = held.tile([P, N], F32, name="sq")
         nc.scalar.activation(sq[:], diff[:], SQUARE)
         rb = held.tile([P, N], BF16, name="rb")

@@ -3,7 +3,6 @@ import concourse.mybir as mybir
 P = 128
 C, S, N, RB = 512, 256, 128, 128
 CB = C // P
-BANK = 512
 
 F32, BF16, U16 = mybir.dt.float32, mybir.dt.bfloat16, mybir.dt.uint16
 ADD, MAX = mybir.AluOpType.add, mybir.AluOpType.max
@@ -24,64 +23,60 @@ def tile_dockingscorepredictor_kernel(tc, x, lig, dist, centers, w1r, b1, w2, b2
         tc.psum_pool(name="psum", bufs=1) as psum,
     ):
         bins_lhsT = held.tile([2, RB], F32, name="bins_lhsT")
-        nc.vector.memset(bins_lhsT[:], 1.0)
+        nc.gpsimd.memset(bins_lhsT[:], 1.0)
         pairs_rhs = held.tile([2, N], F32, name="pairs_rhs")
-        nc.vector.memset(pairs_rhs[:], -1.0)
-        zeros = held.tile([P, BANK], BF16, name="zeros")
-        nc.vector.memset(zeros[:], 0.0)
+        nc.gpsimd.memset(pairs_rhs[:], -1.0)
 
+        nc.sync.dma_start(pairs_rhs[0:1, :], dist)
+        nc.scalar.dma_start(bins_lhsT[1:2, :], centers.rearrange("r o -> o r"))
         offsets = held.tile([P, N // 16], U16, name="offsets")
         nc.sync.dma_start(offsets[:], offs)
-        nc.scalar.dma_start(pairs_rhs[0:1, :], dist)
-        nc.scalar.dma_start(bins_lhsT[1:2, :], centers.rearrange("r o -> o r"))
-        w1r_sb = held.tile([P, C], BF16, name="w1r_sb")
-        nc.scalar.dma_start(w1r_sb[:], w1r)
+        lig_sb = held.tile([P, CB, N], F32, name="lig_sb")
+        nc.sync.dma_start(lig_sb[:], lig.rearrange("(p b) j -> p b j", b=CB))
         x_blocks = x.rearrange("(p b) s -> b p s", b=CB)
         x_sb = [held.tile([P, S], F32, name=f"x_sb{b}") for b in range(CB)]
         nc.sync.dma_start(x_sb[0][:], x_blocks[0])
-        lig_sb = held.tile([P, CB, N], F32, name="lig_sb")
-        nc.scalar.dma_start(lig_sb[:], lig.rearrange("(p b) j -> p b j", b=CB))
+        w1r_sb = held.tile([P, C], BF16, name="w1r_sb")
+        nc.sync.dma_start(w1r_sb[:], w1r)
         for b in range(1, CB):
             nc.sync.dma_start(x_sb[b][:], x_blocks[b])
+        b1_sb = held.tile([P, CB], F32, name="b1_sb")
+        nc.sync.dma_start(b1_sb[:], b1.rearrange("(p b) o -> p (b o)", b=CB))
         w2_blocks = w2.rearrange("(p k) m -> k p m", k=CB)
         w2_sb = [held.tile([P, C], BF16, name=f"w2_sb{k}") for k in range(CB)]
         for k in range(CB):
             nc.sync.dma_start(w2_sb[k][:], w2_blocks[k])
-
-        b1_sb = held.tile([P, CB], F32, name="b1_sb")
-        nc.gpsimd.dma_start(b1_sb[:], b1.rearrange("(p b) o -> p (b o)", b=CB))
         b2_sb = held.tile([P, CB], F32, name="b2_sb")
-        nc.gpsimd.dma_start(b2_sb[:], b2.rearrange("(p b) o -> p (b o)", b=CB))
+        nc.sync.dma_start(b2_sb[:], b2.rearrange("(p b) o -> p (b o)", b=CB))
 
-        unread = psum.tile([P, BANK], F32, name="unread")
-
-        def keep_tensor_engine_busy(matmuls):
-            for i in range(matmuls):
-                nc.tensor.matmul(unread[:], zeros[:, 0:P], zeros[:], start=True, stop=True)
-
-        keep_tensor_engine_busy(3)
-        diff = psum.tile([P, N], F32, name="diff")
+        diff = psum.tile([P, N], F32, name="diff", tag="diff_then_acc0")
         nc.tensor.matmul(diff[:], bins_lhsT[:], pairs_rhs[:], start=True, stop=True)
-        keep_tensor_engine_busy(1)
         sq = held.tile([P, N], F32, name="sq")
         nc.scalar.activation(sq[:], diff[:], SQUARE)
         rb = held.tile([P, N], BF16, name="rb")
         nc.scalar.activation(rb[:], sq[:], EXP, scale=EXP_SCALE)
 
-        w1r_by_block = w1r_sb[:].rearrange("r (p b) -> r b p", b=CB)
-        radial = psum.tile([P, CB, N], F32, name="radial")
+        u = [held.tile([P, N], F32, name=f"u{b}") for b in range(CB)]
         for b in range(CB):
-            nc.tensor.matmul(radial[:, b, :], w1r_by_block[:, b, :], rb[:], start=True, stop=True)
+            nc.vector.tensor_tensor(u[b][:], x_sb[b][:].indirect(offsets[:]), lig_sb[:, b, :], ADD)
 
+        def bias_relu(b, res, acc, bias):
+            if b % 2 == 0:
+                nc.scalar.activation(res, acc, RELU, bias=bias)
+            else:
+                nc.vector.tensor_scalar(res, acc, bias, 0.0, ADD, MAX)
+
+        w1r_by_block = w1r_sb[:].rearrange("r (p b) -> r b p", b=CB)
+        radial = [psum.tile([P, N], F32, name=f"radial{b}") for b in range(CB)]
+        for b in range(CB):
+            nc.tensor.matmul(radial[b][:], w1r_by_block[:, b, :], rb[:], start=True, stop=True)
         h1 = [held.tile([P, N], BF16, name=f"h1_{b}") for b in range(CB)]
         for b in range(CB):
-            u = held.tile([P, N], F32, name=f"u{b}")
-            nc.vector.tensor_tensor(u[:], x_sb[b][:].indirect(offsets[:]), lig_sb[:, b, :], ADD)
             pre = held.tile([P, N], F32, name=f"pre{b}")
-            nc.vector.tensor_tensor(pre[:], radial[:, b, :], u[:], ADD)
+            nc.vector.tensor_tensor(pre[:], radial[b][:], u[b][:], ADD)
             nc.scalar.activation(h1[b][:], pre[:], RELU, bias=b1_sb[:, b : b + 1])
 
-        acc = [psum.tile([P, N], F32, name=f"acc{m}") for m in range(CB)]
+        acc = [psum.tile([P, N], F32, name=f"acc{m}", tag="diff_then_acc0" if m == 0 else f"acc{m}") for m in range(CB)]
         for k in range(CB):
             w2_by_block = w2_sb[k][:].rearrange("c (q m) -> c m q", m=CB)
             for m in range(CB):
@@ -91,7 +86,7 @@ def tile_dockingscorepredictor_kernel(tc, x, lig, dist, centers, w1r, b1, w2, b2
         stores = [nc.sync, nc.scalar]
         for half in range(CB // 2):
             res = held.tile([P, 2, N], F32, name=f"res{half}")
-            m = 2 * half
-            nc.scalar.activation(res[:, 0, :], acc[m][:], RELU, bias=b2_sb[:, m : m + 1])
-            nc.vector.tensor_scalar(res[:, 1, :], acc[m + 1][:], b2_sb[:, m + 1 : m + 2], 0.0, ADD, MAX)
-            stores[half].dma_start(out_blocks[:, m : m + 2, :], res[:])
+            for i in range(2):
+                m = 2 * half + i
+                bias_relu(m, res[:, i, :], acc[m][:], b2_sb[:, m : m + 1])
+            stores[half].dma_start(out_blocks[:, 2 * half : 2 * half + 2, :], res[:])

@@ -26,6 +26,11 @@ def tile_dockingscorepredictor_kernel(tc, x, lig, dist, centers, w1r, b1, w2, b2
         nc.gpsimd.memset(bins_lhsT[:], 1.0)
         pairs_rhs = held.tile([2, N], F32, name="pairs_rhs")
         nc.gpsimd.memset(pairs_rhs[:], -1.0)
+        zeros = held.tile([P, P], BF16, name="zeros")
+        nc.vector.memset(zeros[:], 0.0)
+        unread = psum.tile([P, P], F32, name="unread", tag="unread_then_acc3")
+        for i in range(14):
+            nc.tensor.matmul(unread[:], zeros[:], zeros[:], start=True, stop=True)
 
         nc.sync.dma_start(pairs_rhs[0:1, :], dist)
         nc.scalar.dma_start(bins_lhsT[1:2, :], centers.rearrange("r o -> o r"))
@@ -35,11 +40,11 @@ def tile_dockingscorepredictor_kernel(tc, x, lig, dist, centers, w1r, b1, w2, b2
         nc.sync.dma_start(lig_sb[:], lig.rearrange("(p b) j -> p b j", b=CB))
         x_blocks = x.rearrange("(p b) s -> b p s", b=CB)
         x_sb = [held.tile([P, S], F32, name=f"x_sb{b}") for b in range(CB)]
-        nc.sync.dma_start(x_sb[0][:], x_blocks[0])
+        for b in range(CB - 1):
+            nc.sync.dma_start(x_sb[b][:], x_blocks[b])
         w1r_sb = held.tile([P, C], BF16, name="w1r_sb")
         nc.sync.dma_start(w1r_sb[:], w1r)
-        for b in range(1, CB):
-            nc.sync.dma_start(x_sb[b][:], x_blocks[b])
+        nc.sync.dma_start(x_sb[CB - 1][:], x_blocks[CB - 1])
         b1_sb = held.tile([P, CB], F32, name="b1_sb")
         nc.sync.dma_start(b1_sb[:], b1.rearrange("(p b) o -> p (b o)", b=CB))
         w2_blocks = w2.rearrange("(p k) m -> k p m", k=CB)
@@ -53,6 +58,8 @@ def tile_dockingscorepredictor_kernel(tc, x, lig, dist, centers, w1r, b1, w2, b2
         nc.tensor.matmul(diff[:], bins_lhsT[:], pairs_rhs[:], start=True, stop=True)
         sq = held.tile([P, N], F32, name="sq")
         nc.scalar.activation(sq[:], diff[:], SQUARE)
+        nc.tensor.matmul(unread[:], lig_sb[:, 0, :], lig_sb[:, 0, :], start=True, stop=True)
+        nc.tensor.matmul(unread[:], x_sb[0][:, 0:P], x_sb[0][:, 0:P], start=True, stop=True)
         rb = held.tile([P, N], BF16, name="rb")
         nc.scalar.activation(rb[:], sq[:], EXP, scale=EXP_SCALE)
 
@@ -76,7 +83,8 @@ def tile_dockingscorepredictor_kernel(tc, x, lig, dist, centers, w1r, b1, w2, b2
             nc.vector.tensor_tensor(pre[:], radial[b][:], u[b][:], ADD)
             nc.scalar.activation(h1[b][:], pre[:], RELU, bias=b1_sb[:, b : b + 1])
 
-        acc = [psum.tile([P, N], F32, name=f"acc{m}", tag="diff_then_acc0" if m == 0 else f"acc{m}") for m in range(CB)]
+        acc_tags = ["diff_then_acc0", "acc1", "acc2", "unread_then_acc3"]
+        acc = [psum.tile([P, N], F32, name=f"acc{m}", tag=acc_tags[m]) for m in range(CB)]
         for k in range(CB):
             w2_by_block = w2_sb[k][:].rearrange("c (q m) -> c m q", m=CB)
             for m in range(CB):

@@ -22,18 +22,18 @@ def tile_dockingscorepredictor_kernel(tc, x, lig, dist, centers, w1r, b1, w2, b2
         tc.tile_pool(name="held", bufs=1) as held,
         tc.psum_pool(name="psum", bufs=1) as psum,
     ):
-        bins_lhsT = held.tile([2, RB], F32, name="bins_lhsT")
-        nc.gpsimd.memset(bins_lhsT[:], 1.0)
-        pairs_rhs = held.tile([2, N], F32, name="pairs_rhs")
-        nc.gpsimd.memset(pairs_rhs[:], -1.0)
+        ones = held.tile([1, RB], F32, name="ones")
+        nc.gpsimd.memset(ones[:], 1.0)
         zeros = held.tile([P, P], BF16, name="zeros")
         nc.vector.memset(zeros[:], 0.0)
         unread = psum.tile([P, P], F32, name="unread", tag="unread_then_acc3")
-        for i in range(14):
+        for i in range(12):
             nc.tensor.matmul(unread[:], zeros[:], zeros[:], start=True, stop=True)
 
-        nc.sync.dma_start(pairs_rhs[0:1, :], dist)
-        nc.scalar.dma_start(bins_lhsT[1:2, :], centers.rearrange("r o -> o r"))
+        dist_row = held.tile([1, N], F32, name="dist_row")
+        nc.sync.dma_start(dist_row[:], dist)
+        centers_row = held.tile([1, RB], F32, name="centers_row")
+        nc.scalar.dma_start(centers_row[:], centers.rearrange("r o -> o r"))
         offsets = held.tile([P, N // 16], U16, name="offsets")
         nc.sync.dma_start(offsets[:], offs)
         lig_sb = held.tile([P, CB, N], F32, name="lig_sb")
@@ -54,10 +54,14 @@ def tile_dockingscorepredictor_kernel(tc, x, lig, dist, centers, w1r, b1, w2, b2
         b2_sb = held.tile([P, CB], F32, name="b2_sb")
         nc.sync.dma_start(b2_sb[:], b2.rearrange("(p b) o -> p (b o)", b=CB))
 
-        diff = psum.tile([P, N], F32, name="diff", tag="diff_then_acc0")
-        nc.tensor.matmul(diff[:], bins_lhsT[:], pairs_rhs[:], start=True, stop=True)
+        dist_ps = psum.tile([P, N], F32, name="dist_ps", tag="dist_then_acc0")
+        nc.tensor.matmul(dist_ps[:], ones[:], dist_row[:], start=True, stop=True)
+        centers_ps = psum.tile([P, 1], F32, name="centers_ps", tag="centers_then_acc1")
+        nc.tensor.matmul(centers_ps[:], centers_row[:], ones[:, 0:1], start=True, stop=True)
+        centers_col = held.tile([P, 1], F32, name="centers_col")
+        nc.scalar.copy(centers_col[:], centers_ps[:])
         sq = held.tile([P, N], F32, name="sq")
-        nc.scalar.activation(sq[:], diff[:], SQUARE)
+        nc.scalar.activation(sq[:], dist_ps[:], SQUARE, bias=centers_col[:], scale=-1.0)
         nc.tensor.matmul(unread[:], lig_sb[:, 0, :], lig_sb[:, 0, :], start=True, stop=True)
         nc.tensor.matmul(unread[:], x_sb[0][:, 0:P], x_sb[0][:, 0:P], start=True, stop=True)
         rb = held.tile([P, N], BF16, name="rb")
@@ -83,7 +87,7 @@ def tile_dockingscorepredictor_kernel(tc, x, lig, dist, centers, w1r, b1, w2, b2
             nc.vector.tensor_tensor(pre[:], radial[b][:], u[b][:], ADD)
             nc.scalar.activation(h1[b][:], pre[:], RELU, bias=b1_sb[:, b : b + 1])
 
-        acc_tags = ["diff_then_acc0", "acc1", "acc2", "unread_then_acc3"]
+        acc_tags = ["dist_then_acc0", "centers_then_acc1", "acc2", "unread_then_acc3"]
         acc = [psum.tile([P, N], F32, name=f"acc{m}", tag=acc_tags[m]) for m in range(CB)]
         for k in range(CB):
             w2_by_block = w2_sb[k][:].rearrange("c (q m) -> c m q", m=CB)

@@ -47,10 +47,10 @@ def tile_dockingscorepredictor_kernel(tc, x, lig, dist, centers, w1r, b1, w2, b2
         nc.sync.dma_start(x_sb[CB - 1][:], x_blocks[CB - 1])
         b1_sb = held.tile([P, CB], F32, name="b1_sb")
         nc.sync.dma_start(b1_sb[:], b1.rearrange("(p b) o -> p (b o)", b=CB))
-        w2_blocks = w2.rearrange("(p k) m -> k p m", k=CB)
-        w2_sb = [held.tile([P, C], BF16, name=f"w2_sb{k}") for k in range(CB)]
-        for k in range(CB):
-            nc.sync.dma_start(w2_sb[k][:], w2_blocks[k])
+        w2_halves = w2.rearrange("(p h k) m -> h p k m", h=2, k=CB // 2)
+        w2_sb = [held.tile([P, CB // 2, C], BF16, name=f"w2_sb{h}") for h in range(2)]
+        for h in range(2):
+            nc.sync.dma_start(w2_sb[h][:], w2_halves[h])
         b2_sb = held.tile([P, CB], F32, name="b2_sb")
         nc.sync.dma_start(b2_sb[:], b2.rearrange("(p b) o -> p (b o)", b=CB))
 
@@ -90,7 +90,8 @@ def tile_dockingscorepredictor_kernel(tc, x, lig, dist, centers, w1r, b1, w2, b2
         acc_tags = ["dist_then_acc0", "centers_then_acc1", "acc2", "unread_then_acc3"]
         acc = [psum.tile([P, N], F32, name=f"acc{m}", tag=acc_tags[m]) for m in range(CB)]
         for k in range(CB):
-            w2_by_block = w2_sb[k][:].rearrange("c (q m) -> c m q", m=CB)
+            half, k_in_half = divmod(k, CB // 2)
+            w2_by_block = w2_sb[half][:, k_in_half, :].rearrange("c (q m) -> c m q", m=CB)
             for m in range(CB):
                 nc.tensor.matmul(acc[m][:], w2_by_block[:, m, :], h1[k][:], start=(k == 0), stop=(k == CB - 1))
 

@@ -37,7 +37,7 @@ def tile_dockingscorepredictor_kernel(tc, x, lig, dist, centers, w1r, b1, w2, b2
         offsets = held.tile([P, N // 16], U16, name="offsets")
         nc.sync.dma_start(offsets[:], offs)
         lig_sb = held.tile([P, CB, N], F32, name="lig_sb")
-        nc.sync.dma_start(lig_sb[:], lig.rearrange("(p b) j -> p b j", b=CB))
+        nc.scalar.dma_start(lig_sb[:], lig.rearrange("(p b) j -> p b j", b=CB))
         x_blocks = x.rearrange("(p b) s -> b p s", b=CB)
         x_sb = [held.tile([P, S], F32, name=f"x_sb{b}") for b in range(CB)]
         for b in range(CB - 1):
@@ -49,8 +49,8 @@ def tile_dockingscorepredictor_kernel(tc, x, lig, dist, centers, w1r, b1, w2, b2
         nc.sync.dma_start(b1_sb[:], b1.rearrange("(p b) o -> p (b o)", b=CB))
         w2_halves = w2.rearrange("(p h k) m -> h p k m", h=2, k=CB // 2)
         w2_sb = [held.tile([P, CB // 2, C], BF16, name=f"w2_sb{h}") for h in range(2)]
-        for h in range(2):
-            nc.sync.dma_start(w2_sb[h][:], w2_halves[h])
+        for h, queue in enumerate([nc.scalar, nc.sync]):
+            queue.dma_start(w2_sb[h][:], w2_halves[h])
         b2_sb = held.tile([P, CB], F32, name="b2_sb")
         nc.sync.dma_start(b2_sb[:], b2.rearrange("(p b) o -> p (b o)", b=CB))
 

import concourse.mybir as mybir

P = 128
C, S, N, RB = 512, 256, 128, 128
CB = C // P

F32, BF16, U16 = mybir.dt.float32, mybir.dt.bfloat16, mybir.dt.uint16
ADD, MAX = mybir.AluOpType.add, mybir.AluOpType.max
SQUARE = mybir.ActivationFunctionType.Square
EXP = mybir.ActivationFunctionType.Exp
RELU = mybir.ActivationFunctionType.Relu

BIN_WIDTH = 0.03125 + 1e-8
EXP_SCALE = -0.5 / (BIN_WIDTH * BIN_WIDTH)

FLOPS = 2 * N * (RB * C + C * C)


def tile_dockingscorepredictor_kernel(tc, x, lig, dist, centers, w1r, b1, w2, b2, offs, out):
    nc = tc.nc
    with (
        tc.tile_pool(name="held", bufs=1) as held,
        tc.psum_pool(name="psum", bufs=1) as psum,
    ):
        ones = held.tile([1, RB], F32, name="ones")
        nc.gpsimd.memset(ones[:], 1.0)
        zeros = held.tile([P, P], BF16, name="zeros")
        nc.vector.memset(zeros[:], 0.0)
        unread = psum.tile([P, P], F32, name="unread", tag="unread_then_acc3")
        for i in range(12):
            nc.tensor.matmul(unread[:], zeros[:], zeros[:], start=True, stop=True)

        dist_row = held.tile([1, N], F32, name="dist_row")
        nc.sync.dma_start(dist_row[:], dist)
        centers_row = held.tile([1, RB], F32, name="centers_row")
        nc.scalar.dma_start(centers_row[:], centers.rearrange("r o -> o r"))
        offsets = held.tile([P, N // 16], U16, name="offsets")
        nc.sync.dma_start(offsets[:], offs)
        lig_sb = held.tile([P, CB, N], F32, name="lig_sb")
        nc.scalar.dma_start(lig_sb[:], lig.rearrange("(p b) j -> p b j", b=CB))
        x_blocks = x.rearrange("(p b) s -> b p s", b=CB)
        x_sb = [held.tile([P, S], F32, name=f"x_sb{b}") for b in range(CB)]
        for b in range(CB - 1):
            nc.sync.dma_start(x_sb[b][:], x_blocks[b])
        w1r_sb = held.tile([P, C], BF16, name="w1r_sb")
        nc.sync.dma_start(w1r_sb[:], w1r)
        nc.sync.dma_start(x_sb[CB - 1][:], x_blocks[CB - 1])
        b1_sb = held.tile([P, CB], F32, name="b1_sb")
        nc.sync.dma_start(b1_sb[:], b1.rearrange("(p b) o -> p (b o)", b=CB))
        w2_halves = w2.rearrange("(p h k) m -> h p k m", h=2, k=CB // 2)
        w2_sb = [held.tile([P, CB // 2, C], BF16, name=f"w2_sb{h}") for h in range(2)]
        for h, queue in enumerate([nc.scalar, nc.sync]):
            queue.dma_start(w2_sb[h][:], w2_halves[h])
        b2_sb = held.tile([P, CB], F32, name="b2_sb")
        nc.sync.dma_start(b2_sb[:], b2.rearrange("(p b) o -> p (b o)", b=CB))

        dist_ps = psum.tile([P, N], F32, name="dist_ps", tag="dist_then_acc0")
        nc.tensor.matmul(dist_ps[:], ones[:], dist_row[:], start=True, stop=True)
        centers_ps = psum.tile([P, 1], F32, name="centers_ps", tag="centers_then_acc1")
        nc.tensor.matmul(centers_ps[:], centers_row[:], ones[:, 0:1], start=True, stop=True)
        centers_col = held.tile([P, 1], F32, name="centers_col")
        nc.scalar.copy(centers_col[:], centers_ps[:])
        sq = held.tile([P, N], F32, name="sq")
        nc.scalar.activation(sq[:], dist_ps[:], SQUARE, bias=centers_col[:], scale=-1.0)
        nc.tensor.matmul(unread[:], lig_sb[:, 0, :], lig_sb[:, 0, :], start=True, stop=True)
        nc.tensor.matmul(unread[:], x_sb[0][:, 0:P], x_sb[0][:, 0:P], start=True, stop=True)
        rb = held.tile([P, N], BF16, name="rb")
        nc.scalar.activation(rb[:], sq[:], EXP, scale=EXP_SCALE)

        u = [held.tile([P, N], F32, name=f"u{b}") for b in range(CB)]
        for b in range(CB):
            nc.vector.tensor_tensor(u[b][:], x_sb[b][:].indirect(offsets[:]), lig_sb[:, b, :], ADD)

        def bias_relu(b, res, acc, bias):
            if b % 2 == 0:
                nc.scalar.activation(res, acc, RELU, bias=bias)
            else:
                nc.vector.tensor_scalar(res, acc, bias, 0.0, ADD, MAX)

        w1r_by_block = w1r_sb[:].rearrange("r (p b) -> r b p", b=CB)
        radial = [psum.tile([P, N], F32, name=f"radial{b}") for b in range(CB)]
        for b in range(CB):
            nc.tensor.matmul(radial[b][:], w1r_by_block[:, b, :], rb[:], start=True, stop=True)
        h1 = [held.tile([P, N], BF16, name=f"h1_{b}") for b in range(CB)]
        for b in range(CB):
            pre = held.tile([P, N], F32, name=f"pre{b}")
            nc.vector.tensor_tensor(pre[:], radial[b][:], u[b][:], ADD)
            nc.scalar.activation(h1[b][:], pre[:], RELU, bias=b1_sb[:, b : b + 1])

        acc_tags = ["dist_then_acc0", "centers_then_acc1", "acc2", "unread_then_acc3"]
        acc = [psum.tile([P, N], F32, name=f"acc{m}", tag=acc_tags[m]) for m in range(CB)]
        for k in range(CB):
            half, k_in_half = divmod(k, CB // 2)
            w2_by_block = w2_sb[half][:, k_in_half, :].rearrange("c (q m) -> c m q", m=CB)
            for m in range(CB):
                nc.tensor.matmul(acc[m][:], w2_by_block[:, m, :], h1[k][:], start=(k == 0), stop=(k == CB - 1))

        out_blocks = out.rearrange("(q m) j -> q m j", m=CB)
        stores = [nc.sync, nc.scalar]
        for half in range(CB // 2):
            res = held.tile([P, 2, N], F32, name=f"res{half}")
            for i in range(2):
                m = 2 * half + i
                bias_relu(m, res[:, i, :], acc[m][:], b2_sb[:, m : m + 1])
            stores[half].dma_start(out_blocks[:, 2 * half : 2 * half + 2, :], res[:])
